import numpy as np
import ml_dtypes


def mxq(x, axis, fmt="e4m3"):
    dtype, down = {"e4m3": (ml_dtypes.float8_e4m3fn, 7), "e5m2": (ml_dtypes.float8_e5m2, 14)}[fmt]
    v = np.moveaxis(np.asarray(x, np.float32).astype(ml_dtypes.bfloat16).astype(np.float64), axis, -1)
    blocks = v.reshape(v.shape[:-1] + (-1, 32))
    amax = np.abs(blocks).max(-1, keepdims=True)
    byte = np.maximum(np.where(amax > 0, np.frexp(amax)[1] - 1 + 127, 0) - down, 1)
    scale = np.exp2(byte - 127.0)
    codes = (blocks / scale).astype(np.float32).astype(dtype).astype(np.float64)
    return np.moveaxis((codes * scale).reshape(v.shape), -1, axis)


WIDE = False


def mx_kscale(k):
    if not WIDE:
        return np.ones(k)
    levels = np.array([10, -10, 5, -5, 0])
    a = np.random.permutation(np.resize(levels, k // 512 * 4)).reshape(k // 512, 4)
    idx = np.arange(k)
    return np.exp2(a[idx // 512, idx % 128 // 32])


BF16 = ml_dtypes.bfloat16


def bf(x):
    return np.asarray(x, np.float32).astype(BF16)


def f64(x):
    return np.asarray(x).astype(np.float64)


B, C, PS, G, E = 24, 3, 64, 4, 512
NP = G * G
K2 = 2 * E


def setup_inputs():
    s = mx_kscale(K2)[:E]
    t = mx_kscale(K2)[:E]
    ss = np.concatenate([s, s])
    tt = np.concatenate([t, t])
    return {"tok": bf(np.random.standard_normal((B, NP, E)) * s),
            "corr_w": bf(np.random.standard_normal((E, K2)) / np.sqrt(K2) * t[:, None] / ss[None, :]),
            "corr_b": bf(np.random.standard_normal(E) * 0.3 * t),
            "cross_w": bf(np.random.standard_normal((E, K2)) / np.sqrt(K2) / tt[None, :]),
            "cross_b": bf(np.random.standard_normal(E) * 0.3)}


def reference(tok, corr_w, corr_b, cross_w, cross_b):
    xc = f64(tok)
    a = np.broadcast_to(xc[:, :, None, :], (B, NP, NP, E))
    b = np.broadcast_to(xc[:, None, :, :], (B, NP, NP, E))
    cart = np.concatenate([a, b], axis=-1)
    h = (mxq(cart, 3, "e4m3") @ mxq(f64(corr_w), 1, "e4m3").T) + f64(corr_b)
    h = h.reshape(B, NP, NP // 2, K2)
    return (mxq(h, 3, "e4m3") @ mxq(f64(cross_w), 1, "e4m3").T) + f64(cross_b)

@@ -1,0 +1,240 @@
+from contextlib import ExitStack
+
+import concourse.mybir as mybir
+from concourse.masks import make_identity
+
+F32 = mybir.dt.float32
+BF16 = mybir.dt.bfloat16
+U32 = mybir.dt.uint32
+U8 = mybir.dt.uint8
+FP8X4 = mybir.dt.float8_e4m3fn_x4
+ADD = mybir.AluOpType.add
+
+P = 128
+IMAGES = 24
+TOKENS = 16
+PAIRS = TOKENS // 2
+E = 512
+PACK = 4
+K_PASS = P * PACK
+TOKEN_TILES = IMAGES * TOKENS // P
+IMAGES_PER_TILE = P // TOKENS
+GROUP = 2
+GROUPS = IMAGES // GROUP
+VECTOR_GROUPS = 6
+
+FLOPS = 2 * IMAGES * TOKENS * TOKENS * 2 * E * E + 2 * IMAGES * TOKENS * PAIRS * 2 * E * E
+
+
+def tile_simplemodel_pb_kernel(tc, tok, corr_w, corr_b, cross_w, cross_b, out):
+    nc = tc.nc
+    tok_rows = tok.flatten_outer_dims()
+    out_rows = out.flatten_outer_dims()
+
+    with ExitStack() as stack:
+        keep = stack.enter_context(tc.tile_pool(name="keep", bufs=1))
+        h_pool = stack.enter_context(tc.tile_pool(name="h", bufs=4))
+        out_pool = stack.enter_context(tc.tile_pool(name="o", bufs=4))
+        psum_keep = stack.enter_context(tc.psum_pool(name="psum_keep", bufs=1))
+        psum = stack.enter_context(tc.psum_pool(name="psum", bufs=6))
+
+        tok_sb = keep.tile([P, TOKEN_TILES * E], BF16)
+        nc.sync.dma_start(
+            out=tok_sb[:].rearrange("p (n k) -> p n k", n=TOKEN_TILES),
+            in_=tok_rows.rearrange("(n p) k -> p n k", p=P),
+        )
+        w1_sb = keep.tile([P, PACK * 2 * E], BF16)
+        w1_dram = corr_w.rearrange("(u p e) k -> u p (e k)", u=2, e=2)
+        for u in range(2):
+            nc.sync.dma_start(out=w1_sb[:, u * 4 * E : (u + 1) * 4 * E], in_=w1_dram[u])
+        bias1 = keep.tile([P, PACK], BF16)
+        nc.scalar.dma_start(
+            out=bias1[:].rearrange("p (u e) -> p u e", u=2),
+            in_=corr_b.rearrange("(u p e) -> p u e", u=2, e=2),
+        )
+        w2_sb = keep.tile([P, 4 * 2 * E], BF16)
+        w2_dram = cross_w.rearrange("(n p) k -> p n k", p=P)
+        for half in range(2):
+            nc.sync.dma_start(
+                out=w2_sb[:, half * 4 * E : (half + 1) * 4 * E].rearrange("p (n k) -> p n k", n=2),
+                in_=w2_dram[:, 2 * half : 2 * half + 2, :],
+            )
+        bias2 = keep.tile([P, E], BF16)
+        nc.sync.dma_start(out=bias2[:], in_=cross_b.partition_broadcast(P))
+
+        ident = keep.tile([P, P], F32)
+        make_identity(nc, ident[:])
+
+        def transpose_four(words, first_word):
+            bank = psum.tile([P, 4, P], F32, tag="bank")
+            for s in range(4):
+                nc.tensor.transpose(
+                    bank[:, s, :], words[:, first_word + s * P : first_word + (s + 1) * P], ident[:]
+                )
+            return bank
+
+        tok_words = tok_sb[:].bitcast(F32)
+        tok_grouped = keep.tile([P, TOKEN_TILES * P * PACK], BF16, align_bytes=64)
+        tok_codes = keep.tile([P, TOKEN_TILES * P], U32, align_bytes=64)
+        tok_scales = keep.tile([P, TOKEN_TILES * P], U8, align_bytes=64)
+        for n in range(TOKEN_TILES):
+            bank = psum.tile([P, 2, P], F32, tag="bank")
+            for u in range(2):
+                nc.tensor.transpose(
+                    bank[:, u, :], tok_words[:, (2 * n + u) * P : (2 * n + u + 1) * P], ident[:]
+                )
+            nc.scalar.copy(
+                out=tok_grouped[:, n * K_PASS : (n + 1) * K_PASS]
+                .bitcast(F32)
+                .rearrange("q (r u) -> q r u", u=2),
+                in_=bank[:].rearrange("q u r -> q r u"),
+            )
+            nc.vector.quantize_mx(
+                out=tok_codes[:, n * P : (n + 1) * P].bitcast(FP8X4),
+                scales=tok_scales[:, n * P : (n + 1) * P],
+                in_=tok_grouped[:, n * K_PASS : (n + 1) * K_PASS],
+            )
+
+        w1_words = w1_sb[:].bitcast(F32)
+        w1_grouped = keep.tile([P, PACK * 2 * K_PASS], BF16, align_bytes=64)
+        w1_codes = keep.tile([P, PACK * 2 * P], U32, align_bytes=64)
+        w1_scales = keep.tile([P, PACK * 2 * P], U8, align_bytes=64)
+        for t in range(PACK):
+            bank = transpose_four(w1_words, t * E)
+            nc.scalar.copy(
+                out=w1_grouped[:, t * 2 * K_PASS : (t + 1) * 2 * K_PASS]
+                .bitcast(F32)
+                .rearrange("q (h r u) -> q h r u", h=2, u=2),
+                in_=bank[:].rearrange("q (h u) r -> q h r u", u=2),
+            )
+            nc.vector.quantize_mx(
+                out=w1_codes[:, t * 2 * P : (t + 1) * 2 * P].bitcast(FP8X4),
+                scales=w1_scales[:, t * 2 * P : (t + 1) * 2 * P],
+                in_=w1_grouped[:, t * 2 * K_PASS : (t + 1) * 2 * K_PASS],
+            )
+
+        def token_products(bank, half, n):
+            for t in range(PACK):
+                w_cols = slice((2 * t + half) * P, (2 * t + half + 1) * P)
+                t_cols = slice(n * P, (n + 1) * P)
+                nc.tensor.matmul_mx(
+                    out=bank[:, t, :],
+                    lhsT=w1_codes[:, w_cols].bitcast(FP8X4),
+                    lhsT_scale=w1_scales[:, w_cols],
+                    rhs=tok_codes[:, t_cols].bitcast(FP8X4),
+                    rhs_scale=tok_scales[:, t_cols],
+                    start=True,
+                    stop=True,
+                )
+
+        second = keep.tile([P, IMAGES, 2, PAIRS, PACK], F32)
+        for n in range(TOKEN_TILES):
+            bank = psum.tile([P, PACK, P], F32, tag="bank")
+            token_products(bank, 1, n)
+            for c in range(2):
+                nc.vector.tensor_tensor(
+                    out=second[:, n * IMAGES_PER_TILE : (n + 1) * IMAGES_PER_TILE, c],
+                    in0=bank[:].rearrange("q t (b m c) -> q c b m t", m=PAIRS, c=2)[:, c],
+                    in1=bias1[:]
+                    .unsqueeze(1)
+                    .unsqueeze(1)
+                    .to_broadcast([P, IMAGES_PER_TILE, PAIRS, PACK]),
+                    op=ADD,
+                )
+
+        vector_images = VECTOR_GROUPS * GROUP
+        vector_tiles = (vector_images + IMAGES_PER_TILE - 1) // IMAGES_PER_TILE
+        first_gpsimd_tile = vector_images // IMAGES_PER_TILE
+        first_psum = []
+        for n in range(vector_tiles):
+            bank = psum_keep.tile([P, PACK, P], F32, name="first_psum%d" % n)
+            token_products(bank, 0, n)
+            first_psum.append(bank)
+        first_sbuf = keep.tile([P, TOKEN_TILES * P, PACK], F32)
+        for n in range(first_gpsimd_tile, TOKEN_TILES):
+            bank = psum.tile([P, PACK, P], F32, tag="bank")
+            token_products(bank, 0, n)
+            nc.scalar.copy(
+                out=first_sbuf[:, n * P : (n + 1) * P, :], in_=bank[:].rearrange("q t r -> q r t")
+            )
+
+        w2_words = w2_sb[:].bitcast(F32)
+        w2_grouped = keep.tile([P, 2 * E * PACK], BF16, align_bytes=64)
+        w2_codes = keep.tile([P, 2 * E], U32, align_bytes=64)
+        w2_scales = keep.tile([P, 2 * E], U8, align_bytes=64)
+        for n in range(E // P):
+            bank = transpose_four(w2_words, n * E)
+            nc.scalar.copy(
+                out=w2_grouped[:]
+                .bitcast(F32)
+                .rearrange("q (c n r u) -> q n c r u", c=2, n=E // P, u=2)[:, n],
+                in_=bank[:].rearrange("q (c u) r -> q c r u", u=2),
+            )
+        for c in range(2):
+            nc.vector.quantize_mx(
+                out=w2_codes[:, c * E : (c + 1) * E].bitcast(FP8X4),
+                scales=w2_scales[:, c * E : (c + 1) * E],
+                in_=w2_grouped[:, c * E * PACK : (c + 1) * E * PACK],
+            )
+
+        full = [P, GROUP, TOKENS, PAIRS, PACK]
+
+        def add_group(g):
+            b0 = g * GROUP
+            h_grouped = h_pool.tile([P, GROUP, 2, TOKENS * PAIRS * PACK], BF16, align_bytes=64)
+            if g < VECTOR_GROUPS:
+                engine = nc.vector
+                bank = first_psum[b0 // IMAGES_PER_TILE]
+                t0 = (b0 % IMAGES_PER_TILE) * TOKENS
+                first = bank[:, :, t0 : t0 + GROUP * TOKENS].rearrange("q t (b i) -> q b i t", b=GROUP)
+            else:
+                engine = nc.gpsimd
+                t0 = b0 * TOKENS
+                first = first_sbuf[:, t0 : t0 + GROUP * TOKENS, :].rearrange(
+                    "q (b i) t -> q b i t", b=GROUP
+                )
+            for c in range(2):
+                engine.tensor_tensor(
+                    out=h_grouped[:, :, c, :].rearrange(
+                        "q b (i m t) -> q b i m t", i=TOKENS, m=PAIRS
+                    ),
+                    in0=first.unsqueeze(3).to_broadcast(full),
+                    in1=second[:, b0 : b0 + GROUP, c].unsqueeze(2).to_broadcast(full),
+                    op=ADD,
+                )
+            return h_grouped
+
+        def finish_group(g, h_grouped):
+            b0 = g * GROUP
+            h_codes = h_pool.tile([P, GROUP * 2 * P], U32, align_bytes=64)
+            h_scales = h_pool.tile([P, GROUP * 2 * P], U8, align_bytes=64)
+            nc.vector.quantize_mx(
+                out=h_codes[:].bitcast(FP8X4),
+                scales=h_scales[:],
+                in_=h_grouped[:].rearrange("q b c x -> q (b c x)"),
+            )
+            result = out_pool.tile([P, GROUP, E], F32)
+            for b in range(GROUP):
+                acc = psum.tile([P, E], F32, tag="bank")
+                for c in range(2):
+                    h_cols = slice((2 * b + c) * P, (2 * b + c + 1) * P)
+                    nc.tensor.matmul_mx(
+                        out=acc[:],
+                        lhsT=h_codes[:, h_cols].bitcast(FP8X4),
+                        lhsT_scale=h_scales[:, h_cols],
+                        rhs=w2_codes[:, c * E : (c + 1) * E].bitcast(FP8X4),
+                        rhs_scale=w2_scales[:, c * E : (c + 1) * E],
+                        start=(c == 0),
+                        stop=(c == 1),
+                    )
+                nc.vector.tensor_tensor(out=result[:, b, :], in0=acc[:], in1=bias2[:], op=ADD)
+            nc.sync.dma_start(
+                out=out_rows.rearrange("(b r) e -> r b e", r=P)[:, b0 : b0 + GROUP, :],
+                in_=result[:],
+            )
+
+        for step in range(VECTOR_GROUPS):
+            on_gpsimd = add_group(VECTOR_GROUPS + step)
+            on_vector = add_group(step)
+            finish_group(step, on_vector)
+            finish_group(VECTOR_GROUPS + step, on_gpsimd)

@@ -9,19 +9,23 @@ U32 = mybir.dt.uint32
 U8 = mybir.dt.uint8
 FP8X4 = mybir.dt.float8_e4m3fn_x4
 ADD = mybir.AluOpType.add
+IDENTITY = mybir.ActivationFunctionType.Identity
 
 P = 128
 IMAGES = 24
 TOKENS = 16
 PAIRS = TOKENS // 2
 E = 512
+E_TILES = E // P
 PACK = 4
 K_PASS = P * PACK
 TOKEN_TILES = IMAGES * TOKENS // P
 IMAGES_PER_TILE = P // TOKENS
 GROUP = 2
+GROUP_ROWS = GROUP * P
 GROUPS = IMAGES // GROUP
-VECTOR_GROUPS = 6
+VECTOR_TILES = 2
+VECTOR_GROUPS = VECTOR_TILES * IMAGES_PER_TILE // GROUP
 
 FLOPS = 2 * IMAGES * TOKENS * TOKENS * 2 * E * E + 2 * IMAGES * TOKENS * PAIRS * 2 * E * E
 
@@ -33,8 +37,8 @@ def tile_simplemodel_pb_kernel(tc, tok, corr_w, corr_b, cross_w, cross_b, out):
 
     with ExitStack() as stack:
         keep = stack.enter_context(tc.tile_pool(name="keep", bufs=1))
-        h_pool = stack.enter_context(tc.tile_pool(name="h", bufs=4))
-        out_pool = stack.enter_context(tc.tile_pool(name="o", bufs=4))
+        h_pool = stack.enter_context(tc.tile_pool(name="h", bufs=3))
+        out_pool = stack.enter_context(tc.tile_pool(name="o", bufs=3))
         psum_keep = stack.enter_context(tc.psum_pool(name="psum_keep", bufs=1))
         psum = stack.enter_context(tc.psum_pool(name="psum", bufs=6))
 
@@ -44,23 +48,28 @@ def tile_simplemodel_pb_kernel(tc, tok, corr_w, corr_b, cross_w, cross_b, out):
             in_=tok_rows.rearrange("(n p) k -> p n k", p=P),
         )
         w1_sb = keep.tile([P, PACK * 2 * E], BF16)
-        w1_dram = corr_w.rearrange("(u p e) k -> u p (e k)", u=2, e=2)
-        for u in range(2):
-            nc.sync.dma_start(out=w1_sb[:, u * 4 * E : (u + 1) * 4 * E], in_=w1_dram[u])
-        bias1 = keep.tile([P, PACK], BF16)
-        nc.scalar.dma_start(
-            out=bias1[:].rearrange("p (u e) -> p u e", u=2),
-            in_=corr_b.rearrange("(u p e) -> p u e", u=2, e=2),
-        )
-        w2_sb = keep.tile([P, 4 * 2 * E], BF16)
+        w1_dram = corr_w.rearrange("(u p e) k -> u e p k", u=2, e=2)
+        for t in range(PACK):
+            nc.sync.dma_start(
+                out=w1_sb[:, t * 2 * E : (t + 1) * 2 * E], in_=w1_dram[t // 2, t % 2]
+            )
+        w2_sb = keep.tile([P, E_TILES * 2 * E], BF16)
         w2_dram = cross_w.rearrange("(n p) k -> p n k", p=P)
         for half in range(2):
             nc.sync.dma_start(
                 out=w2_sb[:, half * 4 * E : (half + 1) * 4 * E].rearrange("p (n k) -> p n k", n=2),
                 in_=w2_dram[:, 2 * half : 2 * half + 2, :],
             )
-        bias2 = keep.tile([P, E], BF16)
-        nc.sync.dma_start(out=bias2[:], in_=cross_b.partition_broadcast(P))
+        bias1 = keep.tile([P, PACK], BF16)
+        nc.scalar.dma_start(
+            out=bias1[:].rearrange("p (u e) -> p u e", u=2),
+            in_=corr_b.rearrange("(u p e) -> p u e", u=2, e=2),
+        )
+        bias2_bf = keep.tile([P, E_TILES], BF16)
+        with nc.allow_non_contiguous_dma(reason="512 bias values, one to a partition and tile"):
+            nc.scalar.dma_start(out=bias2_bf[:], in_=cross_b.rearrange("(n p) -> p n", p=P))
+        bias2 = keep.tile([P, E_TILES], F32)
+        nc.vector.tensor_copy(out=bias2[:], in_=bias2_bf[:])
 
         ident = keep.tile([P, P], F32)
         make_identity(nc, ident[:])
@@ -128,7 +137,9 @@ def tile_simplemodel_pb_kernel(tc, tok, corr_w, corr_b, cross_w, cross_b, out):
                 )
 
         second = keep.tile([P, IMAGES, 2, PAIRS, PACK], F32)
-        for n in range(TOKEN_TILES):
+        first_psum = {}
+        first_sbuf = keep.tile([P, P, PACK], F32)
+        for n in (0, 2, 1):
             bank = psum.tile([P, PACK, P], F32, tag="bank")
             token_products(bank, 1, n)
             for c in range(2):
@@ -141,33 +152,25 @@ def tile_simplemodel_pb_kernel(tc, tok, corr_w, corr_b, cross_w, cross_b, out):
                     .to_broadcast([P, IMAGES_PER_TILE, PAIRS, PACK]),
                     op=ADD,
                 )
-
-        vector_images = VECTOR_GROUPS * GROUP
-        vector_tiles = (vector_images + IMAGES_PER_TILE - 1) // IMAGES_PER_TILE
-        first_gpsimd_tile = vector_images // IMAGES_PER_TILE
-        first_psum = []
-        for n in range(vector_tiles):
-            bank = psum_keep.tile([P, PACK, P], F32, name="first_psum%d" % n)
-            token_products(bank, 0, n)
-            first_psum.append(bank)
-        first_sbuf = keep.tile([P, TOKEN_TILES * P, PACK], F32)
-        for n in range(first_gpsimd_tile, TOKEN_TILES):
-            bank = psum.tile([P, PACK, P], F32, tag="bank")
-            token_products(bank, 0, n)
-            nc.scalar.copy(
-                out=first_sbuf[:, n * P : (n + 1) * P, :], in_=bank[:].rearrange("q t r -> q r t")
-            )
+            if n < VECTOR_TILES:
+                bank = psum_keep.tile([P, PACK, P], F32, name="first_psum%d" % n)
+                token_products(bank, 0, n)
+                first_psum[n] = bank
+            else:
+                bank = psum.tile([P, PACK, P], F32, tag="bank")
+                token_products(bank, 0, n)
+                nc.scalar.copy(out=first_sbuf[:], in_=bank[:].rearrange("q t r -> q r t"))
 
         w2_words = w2_sb[:].bitcast(F32)
         w2_grouped = keep.tile([P, 2 * E * PACK], BF16, align_bytes=64)
         w2_codes = keep.tile([P, 2 * E], U32, align_bytes=64)
         w2_scales = keep.tile([P, 2 * E], U8, align_bytes=64)
-        for n in range(E // P):
+        for n in range(E_TILES):
             bank = transpose_four(w2_words, n * E)
             nc.scalar.copy(
                 out=w2_grouped[:]
                 .bitcast(F32)
-                .rearrange("q (c n r u) -> q n c r u", c=2, n=E // P, u=2)[:, n],
+                .rearrange("q (c n r u) -> q n c r u", c=2, n=E_TILES, u=2)[:, n],
                 in_=bank[:].rearrange("q (c u) r -> q c r u", u=2),
             )
         for c in range(2):
@@ -181,60 +184,90 @@ def tile_simplemodel_pb_kernel(tc, tok, corr_w, corr_b, cross_w, cross_b, out):
 
         def add_group(g):
             b0 = g * GROUP
-            h_grouped = h_pool.tile([P, GROUP, 2, TOKENS * PAIRS * PACK], BF16, align_bytes=64)
+            t0 = (b0 % IMAGES_PER_TILE) * TOKENS
             if g < VECTOR_GROUPS:
                 engine = nc.vector
+                h_grouped = h_pool.tile(
+                    [P, 2, GROUP, P * PACK], BF16, align_bytes=64, tag="h_from_vector"
+                )
                 bank = first_psum[b0 // IMAGES_PER_TILE]
-                t0 = (b0 % IMAGES_PER_TILE) * TOKENS
                 first = bank[:, :, t0 : t0 + GROUP * TOKENS].rearrange("q t (b i) -> q b i t", b=GROUP)
             else:
                 engine = nc.gpsimd
-                t0 = b0 * TOKENS
+                h_grouped = h_pool.tile(
+                    [P, 2, GROUP, P * PACK], BF16, align_bytes=64, tag="h_from_gpsimd"
+                )
                 first = first_sbuf[:, t0 : t0 + GROUP * TOKENS, :].rearrange(
                     "q (b i) t -> q b i t", b=GROUP
                 )
             for c in range(2):
                 engine.tensor_tensor(
-                    out=h_grouped[:, :, c, :].rearrange(
-                        "q b (i m t) -> q b i m t", i=TOKENS, m=PAIRS
-                    ),
+                    out=h_grouped[:, c].rearrange("q b (i m t) -> q b i m t", i=TOKENS, m=PAIRS),
                     in0=first.unsqueeze(3).to_broadcast(full),
                     in1=second[:, b0 : b0 + GROUP, c].unsqueeze(2).to_broadcast(full),
                     op=ADD,
                 )
             return h_grouped
 
-        def finish_group(g, h_grouped):
-            b0 = g * GROUP
-            h_codes = h_pool.tile([P, GROUP * 2 * P], U32, align_bytes=64)
-            h_scales = h_pool.tile([P, GROUP * 2 * P], U8, align_bytes=64)
+        def multiply_group(h_grouped):
+            h_codes = h_pool.tile([P, 2 * GROUP_ROWS], U32, align_bytes=64)
+            h_scales = h_pool.tile([P, 2 * GROUP_ROWS], U8, align_bytes=64)
             nc.vector.quantize_mx(
                 out=h_codes[:].bitcast(FP8X4),
                 scales=h_scales[:],
-                in_=h_grouped[:].rearrange("q b c x -> q (b c x)"),
+                in_=h_grouped[:].rearrange("q c b x -> q (c b x)"),
             )
+            out_t = out_pool.tile([P, E_TILES, GROUP_ROWS], F32)
+            for pair in range(E_TILES // 2):
+                acc = psum.tile([P, 2, GROUP_ROWS], F32, tag="bank")
+                for s in range(2):
+                    n = 2 * pair + s
+                    for c in range(2):
+                        w_cols = slice(c * E + n * P, c * E + (n + 1) * P)
+                        h_cols = slice(c * GROUP_ROWS, (c + 1) * GROUP_ROWS)
+                        nc.tensor.matmul_mx(
+                            out=acc[:, s, :],
+                            lhsT=w2_codes[:, w_cols].bitcast(FP8X4),
+                            lhsT_scale=w2_scales[:, w_cols],
+                            rhs=h_codes[:, h_cols].bitcast(FP8X4),
+                            rhs_scale=h_scales[:, h_cols],
+                            start=(c == 0),
+                            stop=(c == 1),
+                        )
+                for s in range(2):
+                    n = 2 * pair + s
+                    nc.scalar.activation(
+                        out=out_t[:, n, :],
+                        in_=acc[:, s, :],
+                        func=IDENTITY,
+                        bias=bias2[:, n : n + 1],
+                        scale=1.0,
+                    )
+            return out_t
+
+        def store_group(g, out_t):
+            b0 = g * GROUP
             result = out_pool.tile([P, GROUP, E], F32)
             for b in range(GROUP):
-                acc = psum.tile([P, E], F32, tag="bank")
-                for c in range(2):
-                    h_cols = slice((2 * b + c) * P, (2 * b + c + 1) * P)
-                    nc.tensor.matmul_mx(
-                        out=acc[:],
-                        lhsT=h_codes[:, h_cols].bitcast(FP8X4),
-                        lhsT_scale=h_scales[:, h_cols],
-                        rhs=w2_codes[:, c * E : (c + 1) * E].bitcast(FP8X4),
-                        rhs_scale=w2_scales[:, c * E : (c + 1) * E],
-                        start=(c == 0),
-                        stop=(c == 1),
-                    )
-                nc.vector.tensor_tensor(out=result[:, b, :], in0=acc[:], in1=bias2[:], op=ADD)
+                back = psum.tile([P, E_TILES, P], F32, tag="bank")
+                for n in range(E_TILES):
+                    nc.tensor.transpose(back[:, n, :], out_t[:, n, b * P : (b + 1) * P], ident[:])
+                nc.scalar.copy(out=result[:, b, :], in_=back[:].rearrange("r n e -> r (n e)"))
             nc.sync.dma_start(
                 out=out_rows.rearrange("(b r) e -> r b e", r=P)[:, b0 : b0 + GROUP, :],
                 in_=result[:],
             )
 
-        for step in range(VECTOR_GROUPS):
-            on_gpsimd = add_group(VECTOR_GROUPS + step)
-            on_vector = add_group(step)
-            finish_group(step, on_vector)
-            finish_group(VECTOR_GROUPS + step, on_gpsimd)
+        order = []
+        for step in range(GROUPS - VECTOR_GROUPS):
+            order.extend([2 * step, 2 * step + 1, VECTOR_GROUPS + step])
+
+        added = {}
+        multiplied = {}
+        for k in range(GROUPS + 2):
+            if k < GROUPS:
+                added[k] = add_group(order[k])
+            if 1 <= k <= GROUPS:
+                multiplied[k - 1] = multiply_group(added[k - 1])
+            if k >= 2:
+                store_group(order[k - 2], multiplied[k - 2])

@@ -26,6 +26,7 @@ GROUP_ROWS = GROUP * P
 GROUPS = IMAGES // GROUP
 VECTOR_TILES = 2
 VECTOR_GROUPS = VECTOR_TILES * IMAGES_PER_TILE // GROUP
+LAG = 2
 
 FLOPS = 2 * IMAGES * TOKENS * TOKENS * 2 * E * E + 2 * IMAGES * TOKENS * PAIRS * 2 * E * E
 
@@ -36,11 +37,12 @@ def tile_simplemodel_pb_kernel(tc, tok, corr_w, corr_b, cross_w, cross_b, out):
     out_rows = out.flatten_outer_dims()
 
     with ExitStack() as stack:
+        stack.enter_context(tc.manual_schedule())
         keep = stack.enter_context(tc.tile_pool(name="keep", bufs=1))
-        h_pool = stack.enter_context(tc.tile_pool(name="h", bufs=3))
+        h_pool = stack.enter_context(tc.tile_pool(name="h", bufs=4))
+        code_pool = stack.enter_context(tc.tile_pool(name="codes", bufs=6))
         out_pool = stack.enter_context(tc.tile_pool(name="o", bufs=3))
         psum_keep = stack.enter_context(tc.psum_pool(name="psum_keep", bufs=1))
-        psum = stack.enter_context(tc.psum_pool(name="psum", bufs=6))
 
         tok_sb = keep.tile([P, TOKEN_TILES * E], BF16)
         nc.sync.dma_start(
@@ -68,169 +70,173 @@ def tile_simplemodel_pb_kernel(tc, tok, corr_w, corr_b, cross_w, cross_b, out):
         bias2_bf = keep.tile([P, E_TILES], BF16)
         with nc.allow_non_contiguous_dma(reason="512 bias values, one to a partition and tile"):
             nc.scalar.dma_start(out=bias2_bf[:], in_=cross_b.rearrange("(n p) -> p n", p=P))
-        bias2 = keep.tile([P, E_TILES], F32)
-        nc.vector.tensor_copy(out=bias2[:], in_=bias2_bf[:])
 
         ident = keep.tile([P, P], F32)
         make_identity(nc, ident[:])
 
-        def transpose_four(words, first_word):
-            bank = psum.tile([P, 4, P], F32, tag="bank")
-            for s in range(4):
-                nc.tensor.transpose(
-                    bank[:, s, :], words[:, first_word + s * P : first_word + (s + 1) * P], ident[:]
-                )
-            return bank
-
-        tok_words = tok_sb[:].bitcast(F32)
         tok_grouped = keep.tile([P, TOKEN_TILES * P * PACK], BF16, align_bytes=64)
         tok_codes = keep.tile([P, TOKEN_TILES * P], U32, align_bytes=64)
         tok_scales = keep.tile([P, TOKEN_TILES * P], U8, align_bytes=64)
-        for n in range(TOKEN_TILES):
-            bank = psum.tile([P, 2, P], F32, tag="bank")
-            for u in range(2):
-                nc.tensor.transpose(
-                    bank[:, u, :], tok_words[:, (2 * n + u) * P : (2 * n + u + 1) * P], ident[:]
-                )
-            nc.scalar.copy(
-                out=tok_grouped[:, n * K_PASS : (n + 1) * K_PASS]
-                .bitcast(F32)
-                .rearrange("q (r u) -> q r u", u=2),
-                in_=bank[:].rearrange("q u r -> q r u"),
-            )
-            nc.vector.quantize_mx(
-                out=tok_codes[:, n * P : (n + 1) * P].bitcast(FP8X4),
-                scales=tok_scales[:, n * P : (n + 1) * P],
-                in_=tok_grouped[:, n * K_PASS : (n + 1) * K_PASS],
-            )
-
-        w1_words = w1_sb[:].bitcast(F32)
         w1_grouped = keep.tile([P, PACK * 2 * K_PASS], BF16, align_bytes=64)
         w1_codes = keep.tile([P, PACK * 2 * P], U32, align_bytes=64)
         w1_scales = keep.tile([P, PACK * 2 * P], U8, align_bytes=64)
-        for t in range(PACK):
-            bank = transpose_four(w1_words, t * E)
-            nc.scalar.copy(
-                out=w1_grouped[:, t * 2 * K_PASS : (t + 1) * 2 * K_PASS]
-                .bitcast(F32)
-                .rearrange("q (h r u) -> q h r u", h=2, u=2),
-                in_=bank[:].rearrange("q (h u) r -> q h r u", u=2),
-            )
-            nc.vector.quantize_mx(
-                out=w1_codes[:, t * 2 * P : (t + 1) * 2 * P].bitcast(FP8X4),
-                scales=w1_scales[:, t * 2 * P : (t + 1) * 2 * P],
-                in_=w1_grouped[:, t * 2 * K_PASS : (t + 1) * 2 * K_PASS],
-            )
-
-        def token_products(bank, half, n):
-            for t in range(PACK):
-                w_cols = slice((2 * t + half) * P, (2 * t + half + 1) * P)
-                t_cols = slice(n * P, (n + 1) * P)
-                nc.tensor.matmul_mx(
-                    out=bank[:, t, :],
-                    lhsT=w1_codes[:, w_cols].bitcast(FP8X4),
-                    lhsT_scale=w1_scales[:, w_cols],
-                    rhs=tok_codes[:, t_cols].bitcast(FP8X4),
-                    rhs_scale=tok_scales[:, t_cols],
-                    start=True,
-                    stop=True,
-                )
-
-        second = keep.tile([P, IMAGES, 2, PAIRS, PACK], F32)
-        first_psum = {}
-        first_sbuf = keep.tile([P, P, PACK], F32)
-        for n in (0, 2, 1):
-            bank = psum.tile([P, PACK, P], F32, tag="bank")
-            token_products(bank, 1, n)
-            for c in range(2):
-                nc.vector.tensor_tensor(
-                    out=second[:, n * IMAGES_PER_TILE : (n + 1) * IMAGES_PER_TILE, c],
-                    in0=bank[:].rearrange("q t (b m c) -> q c b m t", m=PAIRS, c=2)[:, c],
-                    in1=bias1[:]
-                    .unsqueeze(1)
-                    .unsqueeze(1)
-                    .to_broadcast([P, IMAGES_PER_TILE, PAIRS, PACK]),
-                    op=ADD,
-                )
-            if n < VECTOR_TILES:
-                bank = psum_keep.tile([P, PACK, P], F32, name="first_psum%d" % n)
-                token_products(bank, 0, n)
-                first_psum[n] = bank
-            else:
-                bank = psum.tile([P, PACK, P], F32, tag="bank")
-                token_products(bank, 0, n)
-                nc.scalar.copy(out=first_sbuf[:], in_=bank[:].rearrange("q t r -> q r t"))
-
-        w2_words = w2_sb[:].bitcast(F32)
         w2_grouped = keep.tile([P, 2 * E * PACK], BF16, align_bytes=64)
         w2_codes = keep.tile([P, 2 * E], U32, align_bytes=64)
         w2_scales = keep.tile([P, 2 * E], U8, align_bytes=64)
-        for n in range(E_TILES):
-            bank = transpose_four(w2_words, n * E)
+        bias2 = keep.tile([P, E_TILES], F32)
+        second = keep.tile([P, IMAGES, 2, PAIRS, PACK], F32)
+        first_sbuf = keep.tile([P, P, PACK], F32)
+        first_psum = {}
+        for n in range(VECTOR_TILES):
+            first_psum[n] = psum_keep.tile([P, PACK, P], F32, name="first_psum%d" % n)
+
+        with tc.psum_pool(name="psum_head", bufs=1) as psum_head:
+            def transpose_words(words, first_word, count):
+                bank = psum_head.tile([P, count, P], F32, tag="transposed", bufs=2)
+                for s in range(count):
+                    nc.tensor.transpose(
+                        bank[:, s, :],
+                        words[:, first_word + s * P : first_word + (s + 1) * P],
+                        ident[:],
+                    )
+                return bank
+
+            tok_words = tok_sb[:].bitcast(F32)
+            for n in range(TOKEN_TILES):
+                bank = transpose_words(tok_words, n * 2 * P, 2)
+                nc.scalar.copy(
+                    out=tok_grouped[:, n * K_PASS : (n + 1) * K_PASS]
+                    .bitcast(F32)
+                    .rearrange("q (r u) -> q r u", u=2),
+                    in_=bank[:].rearrange("q u r -> q r u"),
+                )
+                nc.vector.quantize_mx(
+                    out=tok_codes[:, n * P : (n + 1) * P].bitcast(FP8X4),
+                    scales=tok_scales[:, n * P : (n + 1) * P],
+                    in_=tok_grouped[:, n * K_PASS : (n + 1) * K_PASS],
+                )
+            nc.scalar.activation(out=bias2[:], in_=bias2_bf[:], func=IDENTITY)
+
+            products = {}
+            for n in range(TOKEN_TILES):
+                products[1, n] = psum_head.tile([P, PACK, P], F32, name="second_psum%d" % n)
+                if n < VECTOR_TILES:
+                    products[0, n] = first_psum[n]
+                else:
+                    products[0, n] = psum_head.tile([P, PACK, P], F32, name="first_psum%d" % n)
+
+            w1_words = w1_sb[:].bitcast(F32)
+            for step in range(PACK + LAG):
+                if step < PACK:
+                    t = step
+                    bank = transpose_words(w1_words, t * E, 4)
+                    nc.scalar.copy(
+                        out=w1_grouped[:, t * 2 * K_PASS : (t + 1) * 2 * K_PASS]
+                        .bitcast(F32)
+                        .rearrange("q (h r u) -> q h r u", h=2, u=2),
+                        in_=bank[:].rearrange("q (h u) r -> q h r u", u=2),
+                    )
+                    nc.vector.quantize_mx(
+                        out=w1_codes[:, t * 2 * P : (t + 1) * 2 * P].bitcast(FP8X4),
+                        scales=w1_scales[:, t * 2 * P : (t + 1) * 2 * P],
+                        in_=w1_grouped[:, t * 2 * K_PASS : (t + 1) * 2 * K_PASS],
+                    )
+                if step >= LAG:
+                    t = step - LAG
+                    for n in (0, 2, 1):
+                        for half in (1, 0):
+                            w_cols = slice((2 * t + half) * P, (2 * t + half + 1) * P)
+                            t_cols = slice(n * P, (n + 1) * P)
+                            nc.tensor.matmul_mx(
+                                out=products[half, n][:, t, :],
+                                lhsT=w1_codes[:, w_cols].bitcast(FP8X4),
+                                lhsT_scale=w1_scales[:, w_cols],
+                                rhs=tok_codes[:, t_cols].bitcast(FP8X4),
+                                rhs_scale=tok_scales[:, t_cols],
+                                start=True,
+                                stop=True,
+                            )
+
+            for n in (0, 2, 1):
+                for c in range(2):
+                    nc.vector.tensor_tensor(
+                        out=second[:, n * IMAGES_PER_TILE : (n + 1) * IMAGES_PER_TILE, c],
+                        in0=products[1, n][:].rearrange("q t (b m c) -> q c b m t", m=PAIRS, c=2)[
+                            :, c
+                        ],
+                        in1=bias1[:]
+                        .unsqueeze(1)
+                        .unsqueeze(1)
+                        .to_broadcast([P, IMAGES_PER_TILE, PAIRS, PACK]),
+                        op=ADD,
+                    )
             nc.scalar.copy(
-                out=w2_grouped[:]
-                .bitcast(F32)
-                .rearrange("q (c n r u) -> q n c r u", c=2, n=E_TILES, u=2)[:, n],
-                in_=bank[:].rearrange("q (c u) r -> q c r u", u=2),
+                out=first_sbuf[:], in_=products[0, VECTOR_TILES][:].rearrange("q t r -> q r t")
             )
-        for c in range(2):
-            nc.vector.quantize_mx(
-                out=w2_codes[:, c * E : (c + 1) * E].bitcast(FP8X4),
-                scales=w2_scales[:, c * E : (c + 1) * E],
-                in_=w2_grouped[:, c * E * PACK : (c + 1) * E * PACK],
-            )
+
+            w2_words = w2_sb[:].bitcast(F32)
+            for n in range(E_TILES):
+                bank = transpose_words(w2_words, n * E, 4)
+                nc.scalar.copy(
+                    out=w2_grouped[:]
+                    .bitcast(F32)
+                    .rearrange("q (c n r u) -> q n c r u", c=2, n=E_TILES, u=2)[:, n],
+                    in_=bank[:].rearrange("q (c u) r -> q c r u", u=2),
+                )
+
+        psum = stack.enter_context(tc.psum_pool(name="psum", bufs=6, reuse_waits="tile"))
 
         full = [P, GROUP, TOKENS, PAIRS, PACK]
 
-        def add_group(g):
+        def add_half(g, c):
             b0 = g * GROUP
             t0 = (b0 % IMAGES_PER_TILE) * TOKENS
             if g < VECTOR_GROUPS:
                 engine = nc.vector
-                h_grouped = h_pool.tile(
-                    [P, 2, GROUP, P * PACK], BF16, align_bytes=64, tag="h_from_vector"
-                )
+                h_grouped = h_pool.tile([P, GROUP, P * PACK], BF16, align_bytes=64, tag="h_vector")
                 bank = first_psum[b0 // IMAGES_PER_TILE]
                 first = bank[:, :, t0 : t0 + GROUP * TOKENS].rearrange("q t (b i) -> q b i t", b=GROUP)
             else:
                 engine = nc.gpsimd
                 h_grouped = h_pool.tile(
-                    [P, 2, GROUP, P * PACK], BF16, align_bytes=64, tag="h_from_gpsimd"
+                    [P, GROUP, P * PACK], BF16, align_bytes=64, tag="h_gpsimd", bufs=1
                 )
                 first = first_sbuf[:, t0 : t0 + GROUP * TOKENS, :].rearrange(
                     "q (b i) t -> q b i t", b=GROUP
                 )
-            for c in range(2):
-                engine.tensor_tensor(
-                    out=h_grouped[:, c].rearrange("q b (i m t) -> q b i m t", i=TOKENS, m=PAIRS),
-                    in0=first.unsqueeze(3).to_broadcast(full),
-                    in1=second[:, b0 : b0 + GROUP, c].unsqueeze(2).to_broadcast(full),
-                    op=ADD,
-                )
+            engine.tensor_tensor(
+                out=h_grouped[:].rearrange("q b (i m t) -> q b i m t", i=TOKENS, m=PAIRS),
+                in0=first.unsqueeze(3).to_broadcast(full),
+                in1=second[:, b0 : b0 + GROUP, c].unsqueeze(2).to_broadcast(full),
+                op=ADD,
+            )
             return h_grouped
 
-        def multiply_group(h_grouped):
-            h_codes = h_pool.tile([P, 2 * GROUP_ROWS], U32, align_bytes=64)
-            h_scales = h_pool.tile([P, 2 * GROUP_ROWS], U8, align_bytes=64)
+        def quantise_half(h_grouped):
+            h_codes = code_pool.tile([P, GROUP_ROWS], U32, align_bytes=64)
+            h_scales = code_pool.tile([P, GROUP_ROWS], U8, align_bytes=64)
             nc.vector.quantize_mx(
                 out=h_codes[:].bitcast(FP8X4),
                 scales=h_scales[:],
-                in_=h_grouped[:].rearrange("q c b x -> q (c b x)"),
+                in_=h_grouped[:].rearrange("q b x -> q (b x)"),
             )
+            return h_codes, h_scales
+
+        def multiply_group(halves):
             out_t = out_pool.tile([P, E_TILES, GROUP_ROWS], F32)
             for pair in range(E_TILES // 2):
                 acc = psum.tile([P, 2, GROUP_ROWS], F32, tag="bank")
                 for s in range(2):
                     n = 2 * pair + s
                     for c in range(2):
+                        h_codes, h_scales = halves[c]
                         w_cols = slice(c * E + n * P, c * E + (n + 1) * P)
-                        h_cols = slice(c * GROUP_ROWS, (c + 1) * GROUP_ROWS)
                         nc.tensor.matmul_mx(
                             out=acc[:, s, :],
                             lhsT=w2_codes[:, w_cols].bitcast(FP8X4),
                             lhsT_scale=w2_scales[:, w_cols],
-                            rhs=h_codes[:, h_cols].bitcast(FP8X4),
-                            rhs_scale=h_scales[:, h_cols],
+                            rhs=h_codes[:].bitcast(FP8X4),
+                            rhs_scale=h_scales[:],
                             start=(c == 0),
                             stop=(c == 1),
                         )
@@ -246,28 +252,34 @@ def tile_simplemodel_pb_kernel(tc, tok, corr_w, corr_b, cross_w, cross_b, out):
             return out_t
 
         def store_group(g, out_t):
-            b0 = g * GROUP
-            result = out_pool.tile([P, GROUP, E], F32)
             for b in range(GROUP):
                 back = psum.tile([P, E_TILES, P], F32, tag="bank")
                 for n in range(E_TILES):
                     nc.tensor.transpose(back[:, n, :], out_t[:, n, b * P : (b + 1) * P], ident[:])
-                nc.scalar.copy(out=result[:, b, :], in_=back[:].rearrange("r n e -> r (n e)"))
-            nc.sync.dma_start(
-                out=out_rows.rearrange("(b r) e -> r b e", r=P)[:, b0 : b0 + GROUP, :],
-                in_=result[:],
-            )
+                result = out_pool.tile([P, E], F32)
+                nc.scalar.copy(out=result[:], in_=back[:].rearrange("r n e -> r (n e)"))
+                row0 = (g * GROUP + b) * P
+                nc.sync.dma_start(out=out_rows[row0 : row0 + P, :], in_=result[:])
 
-        order = []
-        for step in range(GROUPS - VECTOR_GROUPS):
-            order.extend([2 * step, 2 * step + 1, VECTOR_GROUPS + step])
-
-        added = {}
-        multiplied = {}
-        for k in range(GROUPS + 2):
-            if k < GROUPS:
-                added[k] = add_group(order[k])
-            if 1 <= k <= GROUPS:
-                multiplied[k - 1] = multiply_group(added[k - 1])
-            if k >= 2:
-                store_group(order[k - 2], multiplied[k - 2])
+        gpsimd_halves = []
+        previous = None
+        for k in range(VECTOR_GROUPS):
+            from_gpsimd = add_half(VECTOR_GROUPS + k // 2, k % 2)
+            from_vector = [add_half(k, c) for c in range(2)]
+            if k == 0:
+                for c in range(2):
+                    nc.vector.quantize_mx(
+                        out=w2_codes[:, c * E : (c + 1) * E].bitcast(FP8X4),
+                        scales=w2_scales[:, c * E : (c + 1) * E],
+                        in_=w2_grouped[:, c * E * PACK : (c + 1) * E * PACK],
+                    )
+            ready = [(k, [quantise_half(h_grouped) for h_grouped in from_vector])]
+            gpsimd_halves.append(quantise_half(from_gpsimd))
+            if k % 2 == 1:
+                ready.append((VECTOR_GROUPS + k // 2, gpsimd_halves[k - 1 : k + 1]))
+            for g, halves in ready:
+                out_t = multiply_group(halves)
+                if previous is not None:
+                    store_group(previous[0], previous[1])
+                previous = (g, out_t)
+        store_group(previous[0], previous[1])

@@ -41,8 +41,9 @@ def tile_simplemodel_pb_kernel(tc, tok, corr_w, corr_b, cross_w, cross_b, out):
         keep = stack.enter_context(tc.tile_pool(name="keep", bufs=1))
         h_pool = stack.enter_context(tc.tile_pool(name="h", bufs=4))
         code_pool = stack.enter_context(tc.tile_pool(name="codes", bufs=6))
-        out_pool = stack.enter_context(tc.tile_pool(name="o", bufs=3))
+        out_pool = stack.enter_context(tc.tile_pool(name="o", bufs=4))
         psum_keep = stack.enter_context(tc.psum_pool(name="psum_keep", bufs=1))
+        psum = stack.enter_context(tc.psum_pool(name="psum", bufs=4))
 
         tok_sb = keep.tile([P, TOKEN_TILES * E], BF16)
         nc.sync.dma_start(
@@ -73,6 +74,8 @@ def tile_simplemodel_pb_kernel(tc, tok, corr_w, corr_b, cross_w, cross_b, out):
 
         ident = keep.tile([P, P], F32)
         make_identity(nc, ident[:])
+        table_loaded = keep.tile([P, 1], F32)
+        nc.scalar.activation(out=table_loaded[:], in_=ident[:, 0:1], func=IDENTITY)
 
         tok_grouped = keep.tile([P, TOKEN_TILES * P * PACK], BF16, align_bytes=64)
         tok_codes = keep.tile([P, TOKEN_TILES * P], U32, align_bytes=64)
@@ -90,101 +93,108 @@ def tile_simplemodel_pb_kernel(tc, tok, corr_w, corr_b, cross_w, cross_b, out):
         for n in range(VECTOR_TILES):
             first_psum[n] = psum_keep.tile([P, PACK, P], F32, name="first_psum%d" % n)
 
-        with tc.psum_pool(name="psum_head", bufs=1) as psum_head:
-            def transpose_words(words, first_word, count):
-                bank = psum_head.tile([P, count, P], F32, tag="transposed", bufs=2)
-                for s in range(count):
-                    nc.tensor.transpose(
-                        bank[:, s, :],
-                        words[:, first_word + s * P : first_word + (s + 1) * P],
-                        ident[:],
-                    )
-                return bank
-
-            tok_words = tok_sb[:].bitcast(F32)
-            for n in range(TOKEN_TILES):
-                bank = transpose_words(tok_words, n * 2 * P, 2)
-                nc.scalar.copy(
-                    out=tok_grouped[:, n * K_PASS : (n + 1) * K_PASS]
-                    .bitcast(F32)
-                    .rearrange("q (r u) -> q r u", u=2),
-                    in_=bank[:].rearrange("q u r -> q r u"),
+        def transpose_words(words, first_word, count):
+            bank = psum.tile([P, count, P], F32, tag="bank")
+            for s in range(count):
+                nc.tensor.transpose(
+                    bank[:, s, :], words[:, first_word + s * P : first_word + (s + 1) * P], ident[:]
                 )
-                nc.vector.quantize_mx(
-                    out=tok_codes[:, n * P : (n + 1) * P].bitcast(FP8X4),
-                    scales=tok_scales[:, n * P : (n + 1) * P],
-                    in_=tok_grouped[:, n * K_PASS : (n + 1) * K_PASS],
-                )
-            nc.scalar.activation(out=bias2[:], in_=bias2_bf[:], func=IDENTITY)
+            return bank
 
-            products = {}
-            for n in range(TOKEN_TILES):
-                products[1, n] = psum_head.tile([P, PACK, P], F32, name="second_psum%d" % n)
-                if n < VECTOR_TILES:
-                    products[0, n] = first_psum[n]
-                else:
-                    products[0, n] = psum_head.tile([P, PACK, P], F32, name="first_psum%d" % n)
+        tok_words = tok_sb[:].bitcast(F32)
 
-            w1_words = w1_sb[:].bitcast(F32)
-            for step in range(PACK + LAG):
-                if step < PACK:
-                    t = step
-                    bank = transpose_words(w1_words, t * E, 4)
-                    nc.scalar.copy(
-                        out=w1_grouped[:, t * 2 * K_PASS : (t + 1) * 2 * K_PASS]
-                        .bitcast(F32)
-                        .rearrange("q (h r u) -> q h r u", h=2, u=2),
-                        in_=bank[:].rearrange("q (h u) r -> q h r u", u=2),
-                    )
-                    nc.vector.quantize_mx(
-                        out=w1_codes[:, t * 2 * P : (t + 1) * 2 * P].bitcast(FP8X4),
-                        scales=w1_scales[:, t * 2 * P : (t + 1) * 2 * P],
-                        in_=w1_grouped[:, t * 2 * K_PASS : (t + 1) * 2 * K_PASS],
-                    )
-                if step >= LAG:
-                    t = step - LAG
-                    for n in (0, 2, 1):
-                        for half in (1, 0):
-                            w_cols = slice((2 * t + half) * P, (2 * t + half + 1) * P)
-                            t_cols = slice(n * P, (n + 1) * P)
-                            nc.tensor.matmul_mx(
-                                out=products[half, n][:, t, :],
-                                lhsT=w1_codes[:, w_cols].bitcast(FP8X4),
-                                lhsT_scale=w1_scales[:, w_cols],
-                                rhs=tok_codes[:, t_cols].bitcast(FP8X4),
-                                rhs_scale=tok_scales[:, t_cols],
-                                start=True,
-                                stop=True,
-                            )
-
-            for n in (0, 2, 1):
-                for c in range(2):
-                    nc.vector.tensor_tensor(
-                        out=second[:, n * IMAGES_PER_TILE : (n + 1) * IMAGES_PER_TILE, c],
-                        in0=products[1, n][:].rearrange("q t (b m c) -> q c b m t", m=PAIRS, c=2)[
-                            :, c
-                        ],
-                        in1=bias1[:]
-                        .unsqueeze(1)
-                        .unsqueeze(1)
-                        .to_broadcast([P, IMAGES_PER_TILE, PAIRS, PACK]),
-                        op=ADD,
-                    )
+        def prepare_tokens(n):
+            bank = transpose_words(tok_words, n * 2 * P, 2)
             nc.scalar.copy(
-                out=first_sbuf[:], in_=products[0, VECTOR_TILES][:].rearrange("q t r -> q r t")
+                out=tok_grouped[:, n * K_PASS : (n + 1) * K_PASS]
+                .bitcast(F32)
+                .rearrange("q (r u) -> q r u", u=2),
+                in_=bank[:].rearrange("q u r -> q r u"),
+            )
+            nc.vector.quantize_mx(
+                out=tok_codes[:, n * P : (n + 1) * P].bitcast(FP8X4),
+                scales=tok_scales[:, n * P : (n + 1) * P],
+                in_=tok_grouped[:, n * K_PASS : (n + 1) * K_PASS],
             )
 
-            w2_words = w2_sb[:].bitcast(F32)
-            for n in range(E_TILES):
-                bank = transpose_words(w2_words, n * E, 4)
-                nc.scalar.copy(
-                    out=w2_grouped[:]
-                    .bitcast(F32)
-                    .rearrange("q (c n r u) -> q n c r u", c=2, n=E_TILES, u=2)[:, n],
-                    in_=bank[:].rearrange("q (c u) r -> q c r u", u=2),
+        def first_matmul(product, half, n, t):
+            w_cols = slice((2 * t + half) * P, (2 * t + half + 1) * P)
+            t_cols = slice(n * P, (n + 1) * P)
+            nc.tensor.matmul_mx(
+                out=product[:, t, :],
+                lhsT=w1_codes[:, w_cols].bitcast(FP8X4),
+                lhsT_scale=w1_scales[:, w_cols],
+                rhs=tok_codes[:, t_cols].bitcast(FP8X4),
+                rhs_scale=tok_scales[:, t_cols],
+                start=True,
+                stop=True,
+            )
+
+        def second_to_sbuf(product, n):
+            for c in range(2):
+                nc.vector.tensor_tensor(
+                    out=second[:, n * IMAGES_PER_TILE : (n + 1) * IMAGES_PER_TILE, c],
+                    in0=product[:].rearrange("q t (b m c) -> q c b m t", m=PAIRS, c=2)[:, c],
+                    in1=bias1[:]
+                    .unsqueeze(1)
+                    .unsqueeze(1)
+                    .to_broadcast([P, IMAGES_PER_TILE, PAIRS, PACK]),
+                    op=ADD,
                 )
 
-        psum = stack.enter_context(tc.psum_pool(name="psum", bufs=6, reuse_waits="tile"))
+        def prepare_corr_w(t):
+            bank = transpose_words(w1_words, t * E, 4)
+            nc.scalar.copy(
+                out=w1_grouped[:, t * 2 * K_PASS : (t + 1) * 2 * K_PASS]
+                .bitcast(F32)
+                .rearrange("q (h r u) -> q h r u", h=2, u=2),
+                in_=bank[:].rearrange("q (h u) r -> q h r u", u=2),
+            )
+            nc.vector.quantize_mx(
+                out=w1_codes[:, t * 2 * P : (t + 1) * 2 * P].bitcast(FP8X4),
+                scales=w1_scales[:, t * 2 * P : (t + 1) * 2 * P],
+                in_=w1_grouped[:, t * 2 * K_PASS : (t + 1) * 2 * K_PASS],
+            )
+
+        w1_words = w1_sb[:].bitcast(F32)
+        second_psum0 = psum.tile([P, PACK, P], F32, tag="product", bufs=2)
+        prepare_tokens(0)
+        for t in range(PACK):
+            prepare_corr_w(t)
+            if t >= LAG:
+                first_matmul(second_psum0, 1, 0, t - LAG)
+                first_matmul(first_psum[0], 0, 0, t - LAG)
+        prepare_tokens(2)
+        prepare_tokens(1)
+        nc.scalar.activation(out=bias2[:], in_=bias2_bf[:], func=IDENTITY)
+        for t in range(PACK - LAG, PACK):
+            first_matmul(second_psum0, 1, 0, t)
+            first_matmul(first_psum[0], 0, 0, t)
+        second_to_sbuf(second_psum0, 0)
+
+        first_psum2 = psum.tile([P, PACK, P], F32, tag="product", bufs=2)
+        for t in range(PACK):
+            first_matmul(first_psum2, 0, 2, t)
+        nc.scalar.copy(out=first_sbuf[:], in_=first_psum2[:].rearrange("q t r -> q r t"))
+        second_psum2 = psum.tile([P, PACK, P], F32, tag="product", bufs=2)
+        for t in range(PACK):
+            first_matmul(second_psum2, 1, 2, t)
+        second_to_sbuf(second_psum2, 2)
+
+        w2_words = w2_sb[:].bitcast(F32)
+        for n in range(E_TILES):
+            bank = transpose_words(w2_words, n * E, 4)
+            nc.scalar.copy(
+                out=w2_grouped[:]
+                .bitcast(F32)
+                .rearrange("q (c n r u) -> q n c r u", c=2, n=E_TILES, u=2)[:, n],
+                in_=bank[:].rearrange("q (c u) r -> q c r u", u=2),
+            )
+
+        second_psum1 = psum.tile([P, PACK, P], F32, tag="product", bufs=2)
+        for t in range(PACK):
+            first_matmul(second_psum1, 1, 1, t)
+            first_matmul(first_psum[1], 0, 1, t)
 
         full = [P, GROUP, TOKENS, PAIRS, PACK]
 
@@ -251,13 +261,13 @@ def tile_simplemodel_pb_kernel(tc, tok, corr_w, corr_b, cross_w, cross_b, out):
                     )
             return out_t
 
-        def store_group(g, out_t):
+        def store_group(g, out_t, copy):
             for b in range(GROUP):
                 back = psum.tile([P, E_TILES, P], F32, tag="bank")
                 for n in range(E_TILES):
                     nc.tensor.transpose(back[:, n, :], out_t[:, n, b * P : (b + 1) * P], ident[:])
                 result = out_pool.tile([P, E], F32)
-                nc.scalar.copy(out=result[:], in_=back[:].rearrange("r n e -> r (n e)"))
+                copy(out=result[:], in_=back[:].rearrange("r n e -> r (n e)"))
                 row0 = (g * GROUP + b) * P
                 nc.sync.dma_start(out=out_rows[row0 : row0 + P, :], in_=result[:])
 
@@ -277,9 +287,12 @@ def tile_simplemodel_pb_kernel(tc, tok, corr_w, corr_b, cross_w, cross_b, out):
             gpsimd_halves.append(quantise_half(from_gpsimd))
             if k % 2 == 1:
                 ready.append((VECTOR_GROUPS + k // 2, gpsimd_halves[k - 1 : k + 1]))
+            if k == 0:
+                second_to_sbuf(second_psum1, 1)
+            copy = nc.vector.tensor_copy if k == VECTOR_GROUPS - 1 else nc.scalar.copy
             for g, halves in ready:
                 out_t = multiply_group(halves)
                 if previous is not None:
-                    store_group(previous[0], previous[1])
+                    store_group(previous[0], previous[1], copy)
                 previous = (g, out_t)
-        store_group(previous[0], previous[1])
+        store_group(previous[0], previous[1], nc.vector.tensor_copy)

from contextlib import ExitStack

import concourse.mybir as mybir
from concourse.masks import make_identity

F32 = mybir.dt.float32
BF16 = mybir.dt.bfloat16
U32 = mybir.dt.uint32
U8 = mybir.dt.uint8
FP8X4 = mybir.dt.float8_e4m3fn_x4
ADD = mybir.AluOpType.add
IDENTITY = mybir.ActivationFunctionType.Identity

P = 128
IMAGES = 24
TOKENS = 16
PAIRS = TOKENS // 2
E = 512
E_TILES = E // P
PACK = 4
K_PASS = P * PACK
TOKEN_TILES = IMAGES * TOKENS // P
IMAGES_PER_TILE = P // TOKENS
GROUP = 2
GROUP_ROWS = GROUP * P
GROUPS = IMAGES // GROUP
VECTOR_TILES = 2
VECTOR_GROUPS = VECTOR_TILES * IMAGES_PER_TILE // GROUP
LAG = 2

FLOPS = 2 * IMAGES * TOKENS * TOKENS * 2 * E * E + 2 * IMAGES * TOKENS * PAIRS * 2 * E * E


def tile_simplemodel_pb_kernel(tc, tok, corr_w, corr_b, cross_w, cross_b, out):
    nc = tc.nc
    tok_rows = tok.flatten_outer_dims()
    out_rows = out.flatten_outer_dims()

    with ExitStack() as stack:
        stack.enter_context(tc.manual_schedule())
        keep = stack.enter_context(tc.tile_pool(name="keep", bufs=1))
        h_pool = stack.enter_context(tc.tile_pool(name="h", bufs=4))
        code_pool = stack.enter_context(tc.tile_pool(name="codes", bufs=6))
        out_pool = stack.enter_context(tc.tile_pool(name="o", bufs=4))
        psum_keep = stack.enter_context(tc.psum_pool(name="psum_keep", bufs=1))
        psum = stack.enter_context(tc.psum_pool(name="psum", bufs=4))

        tok_sb = keep.tile([P, TOKEN_TILES * E], BF16)
        nc.sync.dma_start(
            out=tok_sb[:].rearrange("p (n k) -> p n k", n=TOKEN_TILES),
            in_=tok_rows.rearrange("(n p) k -> p n k", p=P),
        )
        w1_sb = keep.tile([P, PACK * 2 * E], BF16)
        w1_dram = corr_w.rearrange("(u p e) k -> u e p k", u=2, e=2)
        for t in range(PACK):
            nc.sync.dma_start(
                out=w1_sb[:, t * 2 * E : (t + 1) * 2 * E], in_=w1_dram[t // 2, t % 2]
            )
        w2_sb = keep.tile([P, E_TILES * 2 * E], BF16)
        w2_dram = cross_w.rearrange("(n p) k -> p n k", p=P)
        for half in range(2):
            nc.sync.dma_start(
                out=w2_sb[:, half * 4 * E : (half + 1) * 4 * E].rearrange("p (n k) -> p n k", n=2),
                in_=w2_dram[:, 2 * half : 2 * half + 2, :],
            )
        bias1 = keep.tile([P, PACK], BF16)
        nc.scalar.dma_start(
            out=bias1[:].rearrange("p (u e) -> p u e", u=2),
            in_=corr_b.rearrange("(u p e) -> p u e", u=2, e=2),
        )
        bias2_bf = keep.tile([P, E_TILES], BF16)
        with nc.allow_non_contiguous_dma(reason="512 bias values, one to a partition and tile"):
            nc.scalar.dma_start(out=bias2_bf[:], in_=cross_b.rearrange("(n p) -> p n", p=P))

        ident = keep.tile([P, P], F32)
        make_identity(nc, ident[:])
        table_loaded = keep.tile([P, 1], F32)
        nc.scalar.activation(out=table_loaded[:], in_=ident[:, 0:1], func=IDENTITY)

        tok_grouped = keep.tile([P, TOKEN_TILES * P * PACK], BF16, align_bytes=64)
        tok_codes = keep.tile([P, TOKEN_TILES * P], U32, align_bytes=64)
        tok_scales = keep.tile([P, TOKEN_TILES * P], U8, align_bytes=64)
        w1_grouped = keep.tile([P, PACK * 2 * K_PASS], BF16, align_bytes=64)
        w1_codes = keep.tile([P, PACK * 2 * P], U32, align_bytes=64)
        w1_scales = keep.tile([P, PACK * 2 * P], U8, align_bytes=64)
        w2_grouped = keep.tile([P, 2 * E * PACK], BF16, align_bytes=64)
        w2_codes = keep.tile([P, 2 * E], U32, align_bytes=64)
        w2_scales = keep.tile([P, 2 * E], U8, align_bytes=64)
        bias2 = keep.tile([P, E_TILES], F32)
        second = keep.tile([P, IMAGES, 2, PAIRS, PACK], F32)
        first_sbuf = keep.tile([P, P, PACK], F32)
        first_psum = {}
        for n in range(VECTOR_TILES):
            first_psum[n] = psum_keep.tile([P, PACK, P], F32, name="first_psum%d" % n)

        def transpose_words(words, first_word, count):
            bank = psum.tile([P, count, P], F32, tag="bank")
            for s in range(count):
                nc.tensor.transpose(
                    bank[:, s, :], words[:, first_word + s * P : first_word + (s + 1) * P], ident[:]
                )
            return bank

        tok_words = tok_sb[:].bitcast(F32)

        def prepare_tokens(n):
            bank = transpose_words(tok_words, n * 2 * P, 2)
            nc.scalar.copy(
                out=tok_grouped[:, n * K_PASS : (n + 1) * K_PASS]
                .bitcast(F32)
                .rearrange("q (r u) -> q r u", u=2),
                in_=bank[:].rearrange("q u r -> q r u"),
            )
            nc.vector.quantize_mx(
                out=tok_codes[:, n * P : (n + 1) * P].bitcast(FP8X4),
                scales=tok_scales[:, n * P : (n + 1) * P],
                in_=tok_grouped[:, n * K_PASS : (n + 1) * K_PASS],
            )

        def first_matmul(product, half, n, t):
            w_cols = slice((2 * t + half) * P, (2 * t + half + 1) * P)
            t_cols = slice(n * P, (n + 1) * P)
            nc.tensor.matmul_mx(
                out=product[:, t, :],
                lhsT=w1_codes[:, w_cols].bitcast(FP8X4),
                lhsT_scale=w1_scales[:, w_cols],
                rhs=tok_codes[:, t_cols].bitcast(FP8X4),
                rhs_scale=tok_scales[:, t_cols],
                start=True,
                stop=True,
            )

        def second_to_sbuf(product, n):
            for c in range(2):
                nc.vector.tensor_tensor(
                    out=second[:, n * IMAGES_PER_TILE : (n + 1) * IMAGES_PER_TILE, c],
                    in0=product[:].rearrange("q t (b m c) -> q c b m t", m=PAIRS, c=2)[:, c],
                    in1=bias1[:]
                    .unsqueeze(1)
                    .unsqueeze(1)
                    .to_broadcast([P, IMAGES_PER_TILE, PAIRS, PACK]),
                    op=ADD,
                )

        def prepare_corr_w(t):
            bank = transpose_words(w1_words, t * E, 4)
            nc.scalar.copy(
                out=w1_grouped[:, t * 2 * K_PASS : (t + 1) * 2 * K_PASS]
                .bitcast(F32)
                .rearrange("q (h r u) -> q h r u", h=2, u=2),
                in_=bank[:].rearrange("q (h u) r -> q h r u", u=2),
            )
            nc.vector.quantize_mx(
                out=w1_codes[:, t * 2 * P : (t + 1) * 2 * P].bitcast(FP8X4),
                scales=w1_scales[:, t * 2 * P : (t + 1) * 2 * P],
                in_=w1_grouped[:, t * 2 * K_PASS : (t + 1) * 2 * K_PASS],
            )

        w1_words = w1_sb[:].bitcast(F32)
        second_psum0 = psum.tile([P, PACK, P], F32, tag="product", bufs=2)
        prepare_tokens(0)
        for t in range(PACK):
            prepare_corr_w(t)
            if t >= LAG:
                first_matmul(second_psum0, 1, 0, t - LAG)
                first_matmul(first_psum[0], 0, 0, t - LAG)
        prepare_tokens(2)
        prepare_tokens(1)
        nc.scalar.activation(out=bias2[:], in_=bias2_bf[:], func=IDENTITY)
        for t in range(PACK - LAG, PACK):
            first_matmul(second_psum0, 1, 0, t)
            first_matmul(first_psum[0], 0, 0, t)
        second_to_sbuf(second_psum0, 0)

        first_psum2 = psum.tile([P, PACK, P], F32, tag="product", bufs=2)
        for t in range(PACK):
            first_matmul(first_psum2, 0, 2, t)
        nc.scalar.copy(out=first_sbuf[:], in_=first_psum2[:].rearrange("q t r -> q r t"))
        second_psum2 = psum.tile([P, PACK, P], F32, tag="product", bufs=2)
        for t in range(PACK):
            first_matmul(second_psum2, 1, 2, t)
        second_to_sbuf(second_psum2, 2)

        w2_words = w2_sb[:].bitcast(F32)
        for n in range(E_TILES):
            bank = transpose_words(w2_words, n * E, 4)
            nc.scalar.copy(
                out=w2_grouped[:]
                .bitcast(F32)
                .rearrange("q (c n r u) -> q n c r u", c=2, n=E_TILES, u=2)[:, n],
                in_=bank[:].rearrange("q (c u) r -> q c r u", u=2),
            )

        second_psum1 = psum.tile([P, PACK, P], F32, tag="product", bufs=2)
        for t in range(PACK):
            first_matmul(second_psum1, 1, 1, t)
            first_matmul(first_psum[1], 0, 1, t)

        full = [P, GROUP, TOKENS, PAIRS, PACK]

        def add_half(g, c):
            b0 = g * GROUP
            t0 = (b0 % IMAGES_PER_TILE) * TOKENS
            if g < VECTOR_GROUPS:
                engine = nc.vector
                h_grouped = h_pool.tile([P, GROUP, P * PACK], BF16, align_bytes=64, tag="h_vector")
                bank = first_psum[b0 // IMAGES_PER_TILE]
                first = bank[:, :, t0 : t0 + GROUP * TOKENS].rearrange("q t (b i) -> q b i t", b=GROUP)
            else:
                engine = nc.gpsimd
                h_grouped = h_pool.tile(
                    [P, GROUP, P * PACK], BF16, align_bytes=64, tag="h_gpsimd", bufs=1
                )
                first = first_sbuf[:, t0 : t0 + GROUP * TOKENS, :].rearrange(
                    "q (b i) t -> q b i t", b=GROUP
                )
            engine.tensor_tensor(
                out=h_grouped[:].rearrange("q b (i m t) -> q b i m t", i=TOKENS, m=PAIRS),
                in0=first.unsqueeze(3).to_broadcast(full),
                in1=second[:, b0 : b0 + GROUP, c].unsqueeze(2).to_broadcast(full),
                op=ADD,
            )
            return h_grouped

        def quantise_half(h_grouped):
            h_codes = code_pool.tile([P, GROUP_ROWS], U32, align_bytes=64)
            h_scales = code_pool.tile([P, GROUP_ROWS], U8, align_bytes=64)
            nc.vector.quantize_mx(
                out=h_codes[:].bitcast(FP8X4),
                scales=h_scales[:],
                in_=h_grouped[:].rearrange("q b x -> q (b x)"),
            )
            return h_codes, h_scales

        def multiply_group(halves):
            out_t = out_pool.tile([P, E_TILES, GROUP_ROWS], F32)
            for pair in range(E_TILES // 2):
                acc = psum.tile([P, 2, GROUP_ROWS], F32, tag="bank")
                for s in range(2):
                    n = 2 * pair + s
                    for c in range(2):
                        h_codes, h_scales = halves[c]
                        w_cols = slice(c * E + n * P, c * E + (n + 1) * P)
                        nc.tensor.matmul_mx(
                            out=acc[:, s, :],
                            lhsT=w2_codes[:, w_cols].bitcast(FP8X4),
                            lhsT_scale=w2_scales[:, w_cols],
                            rhs=h_codes[:].bitcast(FP8X4),
                            rhs_scale=h_scales[:],
                            start=(c == 0),
                            stop=(c == 1),
                        )
                for s in range(2):
                    n = 2 * pair + s
                    nc.scalar.activation(
                        out=out_t[:, n, :],
                        in_=acc[:, s, :],
                        func=IDENTITY,
                        bias=bias2[:, n : n + 1],
                        scale=1.0,
                    )
            return out_t

        def store_group(g, out_t, copy):
            for b in range(GROUP):
                back = psum.tile([P, E_TILES, P], F32, tag="bank")
                for n in range(E_TILES):
                    nc.tensor.transpose(back[:, n, :], out_t[:, n, b * P : (b + 1) * P], ident[:])
                result = out_pool.tile([P, E], F32)
                copy(out=result[:], in_=back[:].rearrange("r n e -> r (n e)"))
                row0 = (g * GROUP + b) * P
                nc.sync.dma_start(out=out_rows[row0 : row0 + P, :], in_=result[:])

        gpsimd_halves = []
        previous = None
        for k in range(VECTOR_GROUPS):
            from_gpsimd = add_half(VECTOR_GROUPS + k // 2, k % 2)
            from_vector = [add_half(k, c) for c in range(2)]
            if k == 0:
                for c in range(2):
                    nc.vector.quantize_mx(
                        out=w2_codes[:, c * E : (c + 1) * E].bitcast(FP8X4),
                        scales=w2_scales[:, c * E : (c + 1) * E],
                        in_=w2_grouped[:, c * E * PACK : (c + 1) * E * PACK],
                    )
            ready = [(k, [quantise_half(h_grouped) for h_grouped in from_vector])]
            gpsimd_halves.append(quantise_half(from_gpsimd))
            if k % 2 == 1:
                ready.append((VECTOR_GROUPS + k // 2, gpsimd_halves[k - 1 : k + 1]))
            if k == 0:
                second_to_sbuf(second_psum1, 1)
            copy = nc.vector.tensor_copy if k == VECTOR_GROUPS - 1 else nc.scalar.copy
            for g, halves in ready:
                out_t = multiply_group(halves)
                if previous is not None:
                    store_group(previous[0], previous[1], copy)
                previous = (g, out_t)
        store_group(previous[0], previous[1], nc.vector.tensor_copy)
